import numpy as np
import ml_dtypes


def mxq(x, axis, fmt="e4m3"):
    dtype, down = {"e4m3": (ml_dtypes.float8_e4m3fn, 7), "e5m2": (ml_dtypes.float8_e5m2, 14)}[fmt]
    v = np.moveaxis(np.asarray(x, np.float32).astype(ml_dtypes.bfloat16).astype(np.float64), axis, -1)
    blocks = v.reshape(v.shape[:-1] + (-1, 32))
    amax = np.abs(blocks).max(-1, keepdims=True)
    byte = np.maximum(np.where(amax > 0, np.frexp(amax)[1] - 1 + 127, 0) - down, 1)
    scale = np.exp2(byte - 127.0)
    codes = (blocks / scale).astype(np.float32).astype(dtype).astype(np.float64)
    return np.moveaxis((codes * scale).reshape(v.shape), -1, axis)


WIDE = False


def mx_kscale(k):
    if not WIDE:
        return np.ones(k)
    levels = np.array([10, -10, 5, -5, 0])
    if k % 512:
        return np.exp2(np.random.permutation(np.resize(levels, k // 32))).repeat(32)
    a = np.empty((k // 512, 16))
    for p in range(k // 512):
        a[p, :8] = np.random.permutation(np.resize(levels, 8))
        for g in range(8):
            far = levels[np.abs(levels - a[p, g]) >= 10]
            a[p, g + 8] = far[np.random.randint(len(far))]
    return np.exp2(a.ravel()).repeat(32)


BF16 = ml_dtypes.bfloat16


def bf(x):
    return np.asarray(x, np.float32).astype(BF16)


def f64(x):
    return np.asarray(x).astype(np.float64)


B, C, O, H, W, KT = 2, 512, 512, 32, 40, 7

OFFSETS = ((0, 0), (-1, 0), (1, 0), (0, -1), (0, 1))


def setup_inputs():
    s = mx_kscale(C)
    return {"x": bf(np.random.standard_normal((B, C, H, W)) * s[None, :, None, None]),
            "w": bf(np.random.standard_normal((len(OFFSETS), C, KT, KT)) * 2.0 / s[None, :, None, None]),
            "conv_w": bf(np.random.standard_normal((O, C)) / np.sqrt(C) / s[None, :]),
            "conv_b": bf(np.random.standard_normal(O) * 0.3)}


def reference(x, w, conv_w, conv_b):
    x, w, conv_w, conv_b = f64(x), f64(w), f64(conv_w), f64(conv_b)
    nb_, nc_, hh, ww = x.shape
    k = w.shape[-1]
    ph = k - hh % k
    pw = k - ww % k
    xpd = np.pad(x, ((0, 0), (0, 0), (0, ph), (0, pw)))
    hp, wp = hh + ph, ww + pw
    wpos = np.tile(w, (1, 1, hp // k, wp // k))
    xh = np.pad(xpd, ((0, 0), (0, 0), (1, 1), (1, 1)))
    att = np.zeros_like(xpd)
    for n, (dh, dw) in enumerate(OFFSETS):
        nb = xh[:, :, 1 + dh:1 + dh + hp, 1 + dw:1 + dw + wp]
        att = att + wpos[n][None] * nb
    e = np.exp(att - att.max(axis=1, keepdims=True))
    att = e / e.sum(axis=1, keepdims=True)
    x1 = xpd * att + xpd
    x1 = x1[:, :, :hh, :ww]
    y = np.matmul(mxq(conv_w, 1, "e4m3"), mxq(x1, 1, "e4m3").reshape(nb_, nc_, hh * ww))
    return y.reshape(nb_, -1, hh, ww) + conv_b[None, :, None, None]

@@ -1,0 +1,382 @@
+from contextlib import ExitStack
+
+import concourse.mybir as mybir
+from concourse.masks import make_identity
+
+BF16 = mybir.dt.bfloat16
+F32 = mybir.dt.float32
+I32 = mybir.dt.int32
+U32 = mybir.dt.uint32
+U8 = mybir.dt.uint8
+FP8X4 = mybir.dt.float8_e4m3fn_x4
+ALU = mybir.AluOpType
+ACT = mybir.ActivationFunctionType
+AXIS = mybir.AxisListType
+
+P = 128
+B, C, O, H, W, KT = 2, 512, 512, 32, 40, 7
+CB = C // P
+OB = O // P
+IMG = H * W
+KCOLS = (W + KT - 1) // KT
+WPAD = KCOLS * KT
+MX_N = 512
+ALIGN = 64
+
+OFFSETS = ((0, 0), (-1, 0), (1, 0), (0, -1), (0, 1))
+CENTRE = 0
+SIDE = 4
+VECTOR_TAPS = (3, 1, 2)
+
+FLOPS = 2 * B * IMG * C * O
+
+
+def rows_of(r):
+    return (H - r + KT - 1) // KT
+
+
+def class_size(r):
+    return B * rows_of(r) * KCOLS
+
+
+def group_start(r):
+    return sum(KT * class_size(rr) for rr in range(r))
+
+
+def class_start(r, q):
+    return group_start(r) + q * class_size(r)
+
+
+NPOS = B * H * WPAD
+NTILES = NPOS // P
+SCALAR_LEAD = 2
+CONV_PER_STEP = 2
+W_ROOM = 208
+MAX_CLASSES = 3
+XROOM = (H + KT - 1) * W
+
+
+def tile_lablock_kernel(tc, x, w, conv_w, conv_b, out):
+    nc = tc.nc
+    with ExitStack() as ctx:
+        keep = ctx.enter_context(tc.tile_pool(name="keep", bufs=1))
+        work = ctx.enter_context(tc.tile_pool(name="work", bufs=4))
+        small = ctx.enter_context(tc.tile_pool(name="small", bufs=4))
+        stores = ctx.enter_context(tc.tile_pool(name="stores", bufs=16))
+        psum_setup = ctx.enter_context(tc.psum_pool(name="psum_setup", bufs=1))
+        psum_turn = ctx.enter_context(tc.psum_pool(name="psum_turn", bufs=2))
+        psum_conv = ctx.enter_context(tc.psum_pool(name="psum_conv", bufs=3))
+
+        x_img = keep.tile([P, CB, B, XROOM], BF16)
+        for t in range(CB):
+            nc.sync.dma_start(
+                out=x_img[:, t, :, 0:IMG],
+                in_=x.rearrange("b (p t) i j -> t p b (i j)", t=CB)[t],
+            )
+        w_bf = keep.tile([P, len(OFFSETS), W_ROOM], BF16)
+        nc.scalar.dma_start(
+            out=w_bf[:, :, 0 : CB * KT * KT], in_=w.rearrange("n (p t) r q -> p n (t r q)", p=P)
+        )
+        cw_rows = keep.tile([P, OB, C], BF16)
+        nc.sync.dma_start(out=cw_rows[:], in_=conv_w.rearrange("(ob p) c -> p ob c", p=P))
+        bias_rows = keep.tile([P, P], BF16)
+        nc.vector.memset(bias_rows[:], 0.0)
+        nc.sync.dma_start(out=bias_rows[0:OB, :], in_=conv_b.rearrange("(ob p) -> ob p", p=P))
+
+        ident_f32 = keep.tile([P, P], F32)
+        make_identity(nc, ident_f32[:])
+        ident_bf = keep.tile([P, P], BF16)
+        make_identity(nc, ident_bf[:])
+
+        x_cls = keep.tile([P, CB, NPOS], BF16)
+        nc.vector.memset(x_cls[:].bitcast(I32), 0)
+
+        w_f32 = keep.tile([P, len(OFFSETS) * CB, KT * KT], F32)
+
+        def classes_of(index):
+            return [
+                (r, q)
+                for r in range(KT)
+                for q in range(KT)
+                if index * P <= class_start(r, q) < (index + 1) * P
+            ]
+
+        rows_sorted = set()
+
+        def sort_rows(r):
+            na = rows_of(r)
+            full_q = W - (KCOLS - 1) * KT
+            for t in range(CB):
+                for b in range(B):
+                    src = (
+                        x_img[:, t, b, r * W : r * W + KT * W * na]
+                        .rearrange("p (a z) -> p a z", z=KT * W)[:, :, 0:WPAD]
+                        .rearrange("p a (k q) -> p q a k", q=KT)
+                    )
+                    dst = x_cls[:, t, group_start(r) : group_start(r + 1)].rearrange(
+                        "p (q b a k) -> p q b a k", q=KT, b=B, a=na
+                    )[:, :, b]
+                    pieces = (
+                        (dst[:, 0:full_q], src[:, 0:full_q]),
+                        (dst[:, full_q:KT, :, 0 : KCOLS - 1], src[:, full_q:KT, :, 0 : KCOLS - 1]),
+                    )
+                    for piece_out, piece_in in pieces:
+                        if t % 2 == 0:
+                            nc.vector.tensor_copy(out=piece_out, in_=piece_in)
+                        else:
+                            nc.scalar.copy(out=piece_out, in_=piece_in)
+            rows_sorted.add(r)
+
+        def sort_rows_for(index):
+            for r, q in classes_of(index):
+                for r_read in ((r - 1) % KT, r, (r + 1) % KT):
+                    if r_read not in rows_sorted:
+                        sort_rows(r_read)
+
+        main = keep.tile([P, CB, NPOS], F32)
+        side = keep.tile([P, CB, NPOS], F32)
+        x1_grouped = keep.tile([P, NPOS, CB], BF16, align_bytes=64)
+        x1_codes = keep.tile([P, NPOS], U32, align_bytes=64)
+        x1_scales = keep.tile([P, NPOS], U8, align_bytes=64)
+
+        centre_of = {}
+        logits_t_of = {}
+        neg_max_of = {}
+        gain_of = {}
+        total_of = {}
+        inv_total_of = {}
+        gain_c_of = {}
+        conv_of = {}
+
+        def multiply_on_scalar(index):
+            centre = work.tile([P, MAX_CLASSES, CB, class_size(0)], F32, tag="centre")
+            for slot, (r, q) in enumerate(classes_of(index)):
+                size = class_size(r)
+                start = class_start(r, q)
+                start2 = class_start(r, (q + 1) % KT) + (q + 1) // KT
+                for t in range(CB):
+                    nc.scalar.activation(
+                        out=centre[:, slot, t, 0:size],
+                        in_=x_cls[:, t, start : start + size],
+                        func=ACT.Copy,
+                        scale=w_f32[:, CENTRE * CB + t, r * KT + q : r * KT + q + 1],
+                    )
+                    nc.scalar.activation(
+                        out=side[:, t, start : start + size],
+                        in_=x_cls[:, t, start2 : start2 + size],
+                        func=ACT.Copy,
+                        scale=w_f32[:, SIDE * CB + t, r * KT + q : r * KT + q + 1],
+                    )
+            centre_of[index] = centre
+
+        def add_taps(index):
+            centre = centre_of[index]
+            for tap in VECTOR_TAPS:
+                di, dj = OFFSETS[tap]
+                for slot, (r, q) in enumerate(classes_of(index)):
+                    size = class_size(r)
+                    r2, a_shift = (r + di) % KT, (r + di) // KT
+                    q2, k_shift = (q + dj) % KT, (q + dj) // KT
+                    a_lo = max(0, -a_shift)
+                    a_cnt = min(rows_of(r), rows_of(r2) - a_shift) - a_lo
+                    start = class_start(r, q)
+                    start2 = class_start(r2, q2) + k_shift
+                    for t in range(CB):
+                        acc = main[:, t, start : start + size].rearrange("p (b z) -> p b z", b=B)[
+                            :, :, a_lo * KCOLS : (a_lo + a_cnt) * KCOLS
+                        ]
+                        moved = x_cls[:, t, start2 : start2 + class_size(r2)].rearrange(
+                            "p (b z) -> p b z", b=B
+                        )[:, :, (a_lo + a_shift) * KCOLS : (a_lo + a_shift + a_cnt) * KCOLS]
+                        if tap == VECTOR_TAPS[0]:
+                            before = centre[:, slot, t, 0:size].rearrange("p (b z) -> p b z", b=B)
+                        else:
+                            before = acc
+                        nc.vector.scalar_tensor_tensor(
+                            out=acc,
+                            in0=moved,
+                            scalar=w_f32[:, tap * CB + t, r * KT + q : r * KT + q + 1],
+                            in1=before,
+                            op0=ALU.mult,
+                            op1=ALU.add,
+                        )
+
+        def turn_logits(index):
+            cols = slice(index * P, (index + 1) * P)
+            logits_t = psum_turn.tile([P, CB, P], F32, tag="logits_t")
+            for t in range(CB):
+                nc.tensor.matmul(
+                    out=logits_t[:, t, :], lhsT=main[:, t, cols], rhs=ident_f32[:],
+                    is_transpose=True, start=True, stop=False,
+                )
+                nc.tensor.matmul(
+                    out=logits_t[:, t, :], lhsT=side[:, t, cols], rhs=ident_f32[:],
+                    is_transpose=True, start=False, stop=True,
+                )
+            logits_t_of[index] = logits_t
+
+        def find_max(index):
+            neg_max = small.tile([P, 1], F32, tag="neg_max")
+            nc.vector.tensor_reduce(
+                out=neg_max[:],
+                in_=logits_t_of[index][:].rearrange("p t c -> p (t c)"),
+                axis=AXIS.X,
+                op=ALU.max,
+                negate=True,
+            )
+            neg_max_of[index] = neg_max
+
+        def exponentials(index):
+            gain = work.tile([P, C], F32, tag="gain")
+            total = small.tile([P, 1], F32, tag="total")
+            nc.scalar.activation(
+                out=gain[:],
+                in_=logits_t_of[index][:].rearrange("p t c -> p (t c)"),
+                func=ACT.Exp,
+                bias=neg_max_of[index][:, 0:1],
+                scale=1.0,
+                accum_out=total[:, 0:1],
+            )
+            gain_of[index] = gain
+            total_of[index] = total
+
+        def invert_total(index):
+            inv_total = small.tile([P, 1], F32, tag="inv_total")
+            nc.vector.reciprocal(inv_total[:], total_of[index][:])
+            inv_total_of[index] = inv_total
+
+        def make_gain(index):
+            gain = gain_of[index]
+            nc.scalar.activation(
+                out=gain[:], in_=gain[:], func=ACT.Identity, bias=1.0, scale=inv_total_of[index][:, 0:1]
+            )
+
+        def turn_gain(index):
+            gain_c = psum_turn.tile([P, CB, P], F32, tag="gain_c")
+            for t in range(CB):
+                nc.tensor.transpose(gain_c[:, t, :], gain_of[index][:, t * P : (t + 1) * P], ident_f32[:])
+            gain_c_of[index] = gain_c
+
+        def make_x1(index):
+            cols = slice(index * P, (index + 1) * P)
+            nc.vector.tensor_tensor(
+                out=x1_grouped[:, cols, :],
+                in0=gain_c_of[index][:].rearrange("p t s -> p s t"),
+                in1=x_cls[:, :, cols].rearrange("p t s -> p s t"),
+                op=ALU.mult,
+            )
+            nc.vector.quantize_mx(
+                out=x1_codes[:, cols].bitcast(FP8X4),
+                scales=x1_scales[:, cols],
+                in_=x1_grouped[:, cols, :].rearrange("p s t -> p (s t)"),
+            )
+
+        def window_start(r):
+            end = -(-group_start(r + 1) // ALIGN) * ALIGN
+            return max(0, end - MX_N)
+
+        def convolve(r, ob):
+            first = window_start(r)
+            conv = psum_conv.tile([P, MX_N], F32, tag="conv")
+            nc.tensor.matmul_mx(
+                out=conv[:],
+                lhsT=cw_codes[:, ob * P : (ob + 1) * P].bitcast(FP8X4),
+                lhsT_scale=cw_scales[:, ob * P : (ob + 1) * P],
+                rhs=x1_codes[:, first : first + MX_N].bitcast(FP8X4),
+                rhs_scale=x1_scales[:, first : first + MX_N],
+                start=True,
+                stop=True,
+            )
+            conv_of[(r, ob)] = conv
+
+        def store(r, ob, on_vector):
+            na = rows_of(r)
+            inside = group_start(r) - window_start(r)
+            by_class = conv_of[(r, ob)][:, inside : inside + KT * class_size(r)].rearrange(
+                "p (q b a k) -> p b a k q", q=KT, b=B, a=na
+            )
+            for b in range(B):
+                rows = stores.tile([P, rows_of(0), WPAD], F32, tag="rows")
+                in_order = rows[:, 0:na, :].rearrange("p a (k q) -> p a k q", q=KT)
+                if on_vector:
+                    nc.vector.tensor_scalar(
+                        out=in_order,
+                        in0=by_class[:, b],
+                        scalar1=bias[:, ob : ob + 1],
+                        scalar2=None,
+                        op0=ALU.add,
+                    )
+                else:
+                    nc.scalar.activation(
+                        out=in_order,
+                        in_=by_class[:, b],
+                        func=ACT.Identity,
+                        bias=bias[:, ob : ob + 1],
+                        scale=1.0,
+                    )
+                nc.sync.dma_start(out=out[b, ob * P : (ob + 1) * P, r:H:KT, :], in_=rows[:, 0:na, 0:W])
+
+        cw_codes = keep.tile([P, O], U32, align_bytes=64)
+        cw_scales = keep.tile([P, O], U8, align_bytes=64)
+        bias = keep.tile([P, OB], F32)
+
+        def prepare_conv_w():
+            cw_grouped = keep.tile([P, O, CB], BF16, align_bytes=64)
+            for ob in range(OB):
+                cw_turned = psum_setup.tile([P, CB, P], BF16, tag="setup")
+                for t in range(CB):
+                    nc.tensor.transpose(cw_turned[:, t, :], cw_rows[:, ob, t:C:CB], ident_bf[:])
+                nc.scalar.copy(
+                    out=cw_grouped[:, ob * P : (ob + 1) * P, :],
+                    in_=cw_turned[:].rearrange("p t o -> p o t"),
+                )
+            nc.vector.quantize_mx(
+                out=cw_codes[:].bitcast(FP8X4),
+                scales=cw_scales[:],
+                in_=cw_grouped[:].rearrange("p o t -> p (o t)"),
+            )
+            bias_turned = psum_setup.tile([P, CB, P], BF16, tag="setup")
+            nc.tensor.transpose(bias_turned[:, 0, :], bias_rows[:], ident_bf[:])
+            nc.scalar.copy(out=bias[:], in_=bias_turned[:, 0, 0:OB])
+
+        def running(index):
+            return 0 <= index < NTILES
+
+        sort_rows_for(0)
+        nc.scalar.copy(
+            out=w_f32[:].rearrange("p (n t) z -> p n (t z)", t=CB), in_=w_bf[:, :, 0 : CB * KT * KT]
+        )
+        for index in range(SCALAR_LEAD):
+            sort_rows_for(index)
+            multiply_on_scalar(index)
+        prepare_conv_w()
+        groups_seen = 0
+        waiting = []
+        for step in range(NTILES + 3):
+            blocks = waiting[0:CONV_PER_STEP]
+            waiting = waiting[CONV_PER_STEP:]
+            for r, ob in blocks:
+                convolve(r, ob)
+            if running(step + SCALAR_LEAD):
+                sort_rows_for(step + SCALAR_LEAD)
+                multiply_on_scalar(step + SCALAR_LEAD)
+            for r, ob in blocks:
+                store(r, ob, on_vector=False)
+            if running(step):
+                add_taps(step)
+                turn_logits(step)
+            if running(step - 1):
+                find_max(step - 1)
+                exponentials(step - 1)
+            if running(step - 2):
+                invert_total(step - 2)
+                make_gain(step - 2)
+                turn_gain(step - 2)
+            if running(step - 3):
+                make_x1(step - 3)
+            while groups_seen < KT and window_start(groups_seen) + MX_N <= (step - 2) * P:
+                waiting.extend((groups_seen, ob) for ob in range(OB))
+                groups_seen += 1
+        for r, ob in waiting:
+            convolve(r, ob)
+            store(r, ob, on_vector=(ob % 2 == 1))

@@ -23,10 +23,11 @@ WPAD = KCOLS * KT
 MX_N = 512
 ALIGN = 64
 
-OFFSETS = ((0, 0), (-1, 0), (1, 0), (0, -1), (0, 1))
-CENTRE = 0
-SIDE = 4
-VECTOR_TAPS = (3, 1, 2)
+TAPS = 5
+CENTRE, UP, DOWN, LEFT, RIGHT = range(TAPS)
+VERTICAL = (UP, CENTRE, DOWN)
+HORIZONTAL = (LEFT, RIGHT)
+SLOT = {n: slot for slot, n in enumerate(VERTICAL + HORIZONTAL)}
 
 FLOPS = 2 * B * IMG * C * O
 
@@ -49,10 +50,11 @@ def class_start(r, q):
 
 NPOS = B * H * WPAD
 NTILES = NPOS // P
-SCALAR_LEAD = 2
+LEAD = 2
 CONV_PER_STEP = 2
 W_ROOM = 208
-MAX_CLASSES = 3
+RING = 10 * P
+SCALAR_SORTS = (0, 1)
 XROOM = (H + KT - 1) * W
 
 
@@ -73,7 +75,7 @@ def tile_lablock_kernel(tc, x, w, conv_w, conv_b, out):
                 out=x_img[:, t, :, 0:IMG],
                 in_=x.rearrange("b (p t) i j -> t p b (i j)", t=CB)[t],
             )
-        w_bf = keep.tile([P, len(OFFSETS), W_ROOM], BF16)
+        w_bf = keep.tile([P, TAPS, W_ROOM], BF16)
         nc.scalar.dma_start(
             out=w_bf[:, :, 0 : CB * KT * KT], in_=w.rearrange("n (p t) r q -> p n (t r q)", p=P)
         )
@@ -89,9 +91,14 @@ def tile_lablock_kernel(tc, x, w, conv_w, conv_b, out):
         make_identity(nc, ident_bf[:])
 
         x_cls = keep.tile([P, CB, NPOS], BF16)
-        nc.vector.memset(x_cls[:].bitcast(I32), 0)
+        for t in range(CB):
+            nc.gpsimd.memset(x_cls[:, t].bitcast(I32), 0)
 
-        w_f32 = keep.tile([P, len(OFFSETS) * CB, KT * KT], F32)
+        w_f32 = keep.tile([P, len(HORIZONTAL), CB, KT * KT], F32)
+        w_dup = keep.tile([P, len(VERTICAL), CB * KT * KT, B], BF16)
+
+        def weights_of(n):
+            return w_bf[:, n, 0 : CB * KT * KT]
 
         def classes_of(index):
             return [
@@ -101,45 +108,26 @@ def tile_lablock_kernel(tc, x, w, conv_w, conv_b, out):
                 if index * P <= class_start(r, q) < (index + 1) * P
             ]
 
-        rows_sorted = set()
-
-        def sort_rows(r):
+        def sort_rows(r, t):
+            copy = nc.scalar.copy if t in SCALAR_SORTS else nc.vector.tensor_copy
             na = rows_of(r)
             full_q = W - (KCOLS - 1) * KT
-            for t in range(CB):
-                for b in range(B):
-                    src = (
-                        x_img[:, t, b, r * W : r * W + KT * W * na]
-                        .rearrange("p (a z) -> p a z", z=KT * W)[:, :, 0:WPAD]
-                        .rearrange("p a (k q) -> p q a k", q=KT)
-                    )
-                    dst = x_cls[:, t, group_start(r) : group_start(r + 1)].rearrange(
-                        "p (q b a k) -> p q b a k", q=KT, b=B, a=na
-                    )[:, :, b]
-                    pieces = (
-                        (dst[:, 0:full_q], src[:, 0:full_q]),
-                        (dst[:, full_q:KT, :, 0 : KCOLS - 1], src[:, full_q:KT, :, 0 : KCOLS - 1]),
-                    )
-                    for piece_out, piece_in in pieces:
-                        if t % 2 == 0:
-                            nc.vector.tensor_copy(out=piece_out, in_=piece_in)
-                        else:
-                            nc.scalar.copy(out=piece_out, in_=piece_in)
-            rows_sorted.add(r)
+            for b in range(B):
+                src = (
+                    x_img[:, t, b, r * W : r * W + KT * W * na]
+                    .rearrange("p (a z) -> p a z", z=KT * W)[:, :, 0:WPAD]
+                    .rearrange("p a (k q) -> p q a k", q=KT)
+                )
+                dst = x_cls[:, t, group_start(r) : group_start(r + 1)].rearrange(
+                    "p (q b a k) -> p q b a k", q=KT, b=B, a=na
+                )[:, :, b]
+                copy(out=dst[:, 0:full_q], in_=src[:, 0:full_q])
+                copy(out=dst[:, full_q:KT, :, 0 : KCOLS - 1], in_=src[:, full_q:KT, :, 0 : KCOLS - 1])
 
-        def sort_rows_for(index):
-            for r, q in classes_of(index):
-                for r_read in ((r - 1) % KT, r, (r + 1) % KT):
-                    if r_read not in rows_sorted:
-                        sort_rows(r_read)
-
-        main = keep.tile([P, CB, NPOS], F32)
-        side = keep.tile([P, CB, NPOS], F32)
-        x1_grouped = keep.tile([P, NPOS, CB], BF16, align_bytes=64)
+        products = keep.tile([P, TAPS, CB, RING], F32)
         x1_codes = keep.tile([P, NPOS], U32, align_bytes=64)
         x1_scales = keep.tile([P, NPOS], U8, align_bytes=64)
 
-        centre_of = {}
         logits_t_of = {}
         neg_max_of = {}
         gain_of = {}
@@ -147,72 +135,95 @@ def tile_lablock_kernel(tc, x, w, conv_w, conv_b, out):
         inv_total_of = {}
         gain_c_of = {}
         conv_of = {}
+        x1_of = {}
 
-        def multiply_on_scalar(index):
-            centre = work.tile([P, MAX_CLASSES, CB, class_size(0)], F32, tag="centre")
-            for slot, (r, q) in enumerate(classes_of(index)):
-                size = class_size(r)
-                start = class_start(r, q)
-                start2 = class_start(r, (q + 1) % KT) + (q + 1) // KT
+        def ring_pieces(lo, hi):
+            edge = (lo // RING + 1) * RING
+            return [(lo, hi)] if hi <= edge else [(lo, edge), (edge, hi)]
+
+        def multiply_on_scalar(r, q):
+            sources = {
+                LEFT: class_start(r, (q - 1) % KT) + (q - 1) // KT,
+                RIGHT: class_start(r, (q + 1) % KT) + (q + 1) // KT,
+            }
+            start = class_start(r, q)
+            for lo, hi in ring_pieces(start, start + class_size(r)):
                 for t in range(CB):
-                    nc.scalar.activation(
-                        out=centre[:, slot, t, 0:size],
-                        in_=x_cls[:, t, start : start + size],
-                        func=ACT.Copy,
-                        scale=w_f32[:, CENTRE * CB + t, r * KT + q : r * KT + q + 1],
-                    )
-                    nc.scalar.activation(
-                        out=side[:, t, start : start + size],
-                        in_=x_cls[:, t, start2 : start2 + size],
-                        func=ACT.Copy,
-                        scale=w_f32[:, SIDE * CB + t, r * KT + q : r * KT + q + 1],
-                    )
-            centre_of[index] = centre
-
-        def add_taps(index):
-            centre = centre_of[index]
-            for tap in VECTOR_TAPS:
-                di, dj = OFFSETS[tap]
-                for slot, (r, q) in enumerate(classes_of(index)):
-                    size = class_size(r)
-                    r2, a_shift = (r + di) % KT, (r + di) // KT
-                    q2, k_shift = (q + dj) % KT, (q + dj) // KT
-                    a_lo = max(0, -a_shift)
-                    a_cnt = min(rows_of(r), rows_of(r2) - a_shift) - a_lo
-                    start = class_start(r, q)
-                    start2 = class_start(r2, q2) + k_shift
-                    for t in range(CB):
-                        acc = main[:, t, start : start + size].rearrange("p (b z) -> p b z", b=B)[
-                            :, :, a_lo * KCOLS : (a_lo + a_cnt) * KCOLS
-                        ]
-                        moved = x_cls[:, t, start2 : start2 + class_size(r2)].rearrange(
-                            "p (b z) -> p b z", b=B
-                        )[:, :, (a_lo + a_shift) * KCOLS : (a_lo + a_shift + a_cnt) * KCOLS]
-                        if tap == VECTOR_TAPS[0]:
-                            before = centre[:, slot, t, 0:size].rearrange("p (b z) -> p b z", b=B)
-                        else:
-                            before = acc
-                        nc.vector.scalar_tensor_tensor(
-                            out=acc,
-                            in0=moved,
-                            scalar=w_f32[:, tap * CB + t, r * KT + q : r * KT + q + 1],
-                            in1=before,
-                            op0=ALU.mult,
-                            op1=ALU.add,
+                    for slot, n in enumerate(HORIZONTAL):
+                        at = sources[n] + lo - start
+                        nc.scalar.activation(
+                            out=products[:, SLOT[n], t, lo % RING : lo % RING + hi - lo],
+                            in_=x_cls[:, t, at : at + hi - lo],
+                            func=ACT.Copy,
+                            scale=w_f32[:, slot, t, r * KT + q : r * KT + q + 1],
                         )
 
+        def unit(r):
+            return rows_of(r) * KCOLS
+
+        def parts_of_group(r):
+            size = unit(r)
+            cut = RING - group_start(r) % RING
+            if cut >= KT * class_size(r):
+                return [(0, KT * B, 0, size)]
+            h, z = divmod(cut, size)
+            parts = [(0, h, 0, size), (h, 1, 0, z), (h, 1, z, size), (h + 1, KT * B - h - 1, 0, size)]
+            return [part for part in parts if part[1] > 0 and part[2] < part[3]]
+
+        def columns(tile, ts, start, count, size, lo, hi):
+            if count == 1:
+                return tile[:, ts, start + lo : start + hi]
+            return tile[:, ts, start : start + count * size].rearrange("p t (h z) -> p t h z", z=size)[:, :, :, lo:hi]
+
+        def vector_products(r):
+            size = unit(r)
+            jobs = []
+            for n, step in ((UP, -1), (CENTRE, 0), (DOWN, 1)):
+                r2 = (r + step) % KT
+                moved = (r + step) // KT * KCOLS
+                product = products[:, SLOT[n]]
+                w_rows = w_dup[:, SLOT[n]].rearrange("p (t r q) b -> p t r (q b)", t=CB, r=KT)
+                inside_lo, inside_hi = max(0, -moved), min(size, unit(r2) - moved)
+                for h, count, z_lo, z_hi in parts_of_group(r):
+                    at = (group_start(r) + h * size + z_lo) % RING - z_lo
+                    at2 = group_start(r2) + h * unit(r2)
+                    lo, hi = max(z_lo, inside_lo), min(z_hi, inside_hi)
+                    for t in range(0, CB, 2):
+                        ts = slice(t, t + 2)
+                        weights = w_rows[:, ts, r, h : h + count]
+                        if count == 1:
+                            weights = weights.to_broadcast([P, 2, hi - lo])
+                        else:
+                            weights = weights.unsqueeze(3).to_broadcast([P, 2, count, hi - lo])
+                        for lo_out, hi_out in ((z_lo, min(z_hi, inside_lo)), (max(z_lo, inside_hi), z_hi)):
+                            if lo_out < hi_out:
+                                jobs.append((columns(product, ts, at, count, size, lo_out, hi_out), None, None))
+                        if lo < hi:
+                            jobs.append(
+                                (
+                                    columns(product, ts, at, count, size, lo, hi),
+                                    columns(x_cls, ts, at2, count, unit(r2), lo + moved, hi + moved),
+                                    weights,
+                                )
+                            )
+            return jobs
+
+        def multiply_on_vector(job):
+            product, x_moved, weights = job
+            if weights is None:
+                nc.vector.memset(product, 0.0)
+            else:
+                nc.vector.tensor_tensor(out=product, in0=x_moved, in1=weights, op=ALU.mult)
+
         def turn_logits(index):
-            cols = slice(index * P, (index + 1) * P)
+            at = index * P % RING
             logits_t = psum_turn.tile([P, CB, P], F32, tag="logits_t")
             for t in range(CB):
-                nc.tensor.matmul(
-                    out=logits_t[:, t, :], lhsT=main[:, t, cols], rhs=ident_f32[:],
-                    is_transpose=True, start=True, stop=False,
-                )
-                nc.tensor.matmul(
-                    out=logits_t[:, t, :], lhsT=side[:, t, cols], rhs=ident_f32[:],
-                    is_transpose=True, start=False, stop=True,
-                )
+                for slot in range(TAPS):
+                    nc.tensor.matmul(
+                        out=logits_t[:, t, :], lhsT=products[:, slot, t, at : at + P], rhs=ident_f32[:],
+                        is_transpose=True, start=(slot == 0), stop=(slot == TAPS - 1),
+                    )
             logits_t_of[index] = logits_t
 
         def find_max(index):
@@ -247,8 +258,13 @@ def tile_lablock_kernel(tc, x, w, conv_w, conv_b, out):
 
         def make_gain(index):
             gain = gain_of[index]
-            nc.scalar.activation(
-                out=gain[:], in_=gain[:], func=ACT.Identity, bias=1.0, scale=inv_total_of[index][:, 0:1]
+            nc.gpsimd.tensor_scalar(
+                out=gain[:],
+                in0=gain[:],
+                scalar1=inv_total_of[index][:, 0:1],
+                scalar2=1.0,
+                op0=ALU.mult,
+                op1=ALU.add,
             )
 
         def turn_gain(index):
@@ -259,16 +275,21 @@ def tile_lablock_kernel(tc, x, w, conv_w, conv_b, out):
 
         def make_x1(index):
             cols = slice(index * P, (index + 1) * P)
+            x1_grouped = work.tile([P, P, CB], BF16, tag="x1_grouped", align_bytes=64)
             nc.vector.tensor_tensor(
-                out=x1_grouped[:, cols, :],
+                out=x1_grouped[:],
                 in0=gain_c_of[index][:].rearrange("p t s -> p s t"),
                 in1=x_cls[:, :, cols].rearrange("p t s -> p s t"),
                 op=ALU.mult,
             )
+            x1_of[index] = x1_grouped
+
+        def quantise(index):
+            cols = slice(index * P, (index + 1) * P)
             nc.vector.quantize_mx(
                 out=x1_codes[:, cols].bitcast(FP8X4),
                 scales=x1_scales[:, cols],
-                in_=x1_grouped[:, cols, :].rearrange("p s t -> p (s t)"),
+                in_=x1_of[index][:].rearrange("p s t -> p (s t)"),
             )
 
         def window_start(r):
@@ -320,63 +341,95 @@ def tile_lablock_kernel(tc, x, w, conv_w, conv_b, out):
         cw_scales = keep.tile([P, O], U8, align_bytes=64)
         bias = keep.tile([P, OB], F32)
 
-        def prepare_conv_w():
-            cw_grouped = keep.tile([P, O, CB], BF16, align_bytes=64)
-            for ob in range(OB):
-                cw_turned = psum_setup.tile([P, CB, P], BF16, tag="setup")
-                for t in range(CB):
-                    nc.tensor.transpose(cw_turned[:, t, :], cw_rows[:, ob, t:C:CB], ident_bf[:])
-                nc.scalar.copy(
-                    out=cw_grouped[:, ob * P : (ob + 1) * P, :],
-                    in_=cw_turned[:].rearrange("p t o -> p o t"),
-                )
+        cw_grouped = keep.tile([P, O, CB], BF16, align_bytes=64)
+
+        def turn_conv_w(ob):
+            cw_turned = psum_setup.tile([P, CB, P], BF16, tag="setup", name="cw_turned")
+            for t in range(CB):
+                nc.tensor.transpose(cw_turned[:, t, :], cw_rows[:, ob, t:C:CB], ident_bf[:])
+            nc.scalar.copy(
+                out=cw_grouped[:, ob * P : (ob + 1) * P, :], in_=cw_turned[:].rearrange("p t o -> p o t")
+            )
+
+        def quantise_conv_w():
             nc.vector.quantize_mx(
                 out=cw_codes[:].bitcast(FP8X4),
                 scales=cw_scales[:],
                 in_=cw_grouped[:].rearrange("p o t -> p (o t)"),
             )
-            bias_turned = psum_setup.tile([P, CB, P], BF16, tag="setup")
+
+        def turn_bias():
+            bias_turned = psum_setup.tile([P, CB, P], BF16, tag="setup", name="bias_turned")
             nc.tensor.transpose(bias_turned[:, 0, :], bias_rows[:], ident_bf[:])
             nc.scalar.copy(out=bias[:], in_=bias_turned[:, 0, 0:OB])
 
         def running(index):
             return 0 <= index < NTILES
 
-        sort_rows_for(0)
-        nc.scalar.copy(
-            out=w_f32[:].rearrange("p (n t) z -> p n (t z)", t=CB), in_=w_bf[:, :, 0 : CB * KT * KT]
-        )
-        for index in range(SCALAR_LEAD):
-            sort_rows_for(index)
-            multiply_on_scalar(index)
-        prepare_conv_w()
-        groups_seen = 0
-        waiting = []
-        for step in range(NTILES + 3):
-            blocks = waiting[0:CONV_PER_STEP]
-            waiting = waiting[CONV_PER_STEP:]
-            for r, ob in blocks:
+        for slot, n in enumerate(HORIZONTAL):
+            nc.scalar.copy(out=w_f32[:, slot].rearrange("p t z -> p (t z)"), in_=weights_of(n))
+        for slot, n in enumerate(VERTICAL):
+            nc.vector.tensor_copy(
+                out=w_dup[:, slot], in_=weights_of(n).unsqueeze(2).to_broadcast([P, CB * KT * KT, B])
+            )
+
+        sorts, products_at = {}, {}
+        for r in range(KT):
+            first = group_start(r) // P
+            jobs = vector_products(r)
+            for k, job in enumerate(jobs):
+                products_at.setdefault(first - 3 + 3 * k // len(jobs), []).append(job)
+            for r_new in (KT - 1, 0, 1) if r == 0 else (r + 1,) if r + 1 < KT - 1 else ():
+                for t in range(CB):
+                    sorts.setdefault(first - 6 + min(t, 2), []).append((r_new, t))
+
+        def prepare(step):
+            for r, t in sorts.get(step, []):
+                sort_rows(r, t)
+            for r, q in classes_of(step + LEAD):
+                multiply_on_scalar(r, q)
+
+        def multiply(step, half):
+            jobs = products_at.get(step, [])
+            middle = (len(jobs) + 1) // 2
+            for job in jobs[:middle] if half == 0 else jobs[middle:]:
+                multiply_on_vector(job)
+
+        with tc.manual_schedule():
+            groups_seen = 0
+            waiting = []
+            for step in range(-6, NTILES + 5):
+                blocks = waiting[0:CONV_PER_STEP]
+                waiting = waiting[CONV_PER_STEP:]
+                if running(step - 2):
+                    invert_total(step - 2)
+                    make_gain(step - 2)
+                if running(step - 1):
+                    find_max(step - 1)
+                    exponentials(step - 1)
+                for r, ob in blocks:
+                    convolve(r, ob)
+                    store(r, ob, on_vector=False)
+                if step == OB + 1:
+                    quantise_conv_w()
+                if running(step - 4):
+                    quantise(step - 4)
+                prepare(step)
+                multiply(step, 0)
+                if running(step - 3):
+                    make_x1(step - 3)
+                multiply(step, 1)
+                if running(step):
+                    turn_logits(step)
+                if running(step - 2):
+                    turn_gain(step - 2)
+                if 0 <= step - 1 < OB:
+                    turn_conv_w(step - 1)
+                if step == OB + 1:
+                    turn_bias()
+                while groups_seen < KT and window_start(groups_seen) + MX_N <= (step - 3) * P:
+                    waiting.extend((groups_seen, ob) for ob in range(OB))
+                    groups_seen += 1
+            for r, ob in waiting:
                 convolve(r, ob)
-            if running(step + SCALAR_LEAD):
-                sort_rows_for(step + SCALAR_LEAD)
-                multiply_on_scalar(step + SCALAR_LEAD)
-            for r, ob in blocks:
-                store(r, ob, on_vector=False)
-            if running(step):
-                add_taps(step)
-                turn_logits(step)
-            if running(step - 1):
-                find_max(step - 1)
-                exponentials(step - 1)
-            if running(step - 2):
-                invert_total(step - 2)
-                make_gain(step - 2)
-                turn_gain(step - 2)
-            if running(step - 3):
-                make_x1(step - 3)
-            while groups_seen < KT and window_start(groups_seen) + MX_N <= (step - 2) * P:
-                waiting.extend((groups_seen, ob) for ob in range(OB))
-                groups_seen += 1
-        for r, ob in waiting:
-            convolve(r, ob)
-            store(r, ob, on_vector=(ob % 2 == 1))
+                store(r, ob, on_vector=(ob % 2 == 1))

@@ -25,9 +25,12 @@ ALIGN = 64
 
 TAPS = 5
 CENTRE, UP, DOWN, LEFT, RIGHT = range(TAPS)
-VERTICAL = (UP, CENTRE, DOWN)
-HORIZONTAL = (LEFT, RIGHT)
-SLOT = {n: slot for slot, n in enumerate(VERTICAL + HORIZONTAL)}
+BASE = LEFT
+ADDED = (CENTRE, UP)
+SIDE = RIGHT
+WHOLE = DOWN
+SHORT = (BASE, SIDE) + ADDED
+SLOTS = {WHOLE: 0, BASE: 1, SIDE: 2}
 
 FLOPS = 2 * B * IMG * C * O
 
@@ -54,7 +57,9 @@ LEAD = 2
 CONV_PER_STEP = 2
 W_ROOM = 208
 RING = 10 * P
-SCALAR_SORTS = (0, 1)
+SCALAR_SORTS = (1, 3)
+SCALAR_LATE = 2
+NEAR = 4
 XROOM = (H + KT - 1) * W
 
 
@@ -64,7 +69,7 @@ def tile_lablock_kernel(tc, x, w, conv_w, conv_b, out):
         keep = ctx.enter_context(tc.tile_pool(name="keep", bufs=1))
         work = ctx.enter_context(tc.tile_pool(name="work", bufs=4))
         small = ctx.enter_context(tc.tile_pool(name="small", bufs=4))
-        stores = ctx.enter_context(tc.tile_pool(name="stores", bufs=16))
+        stores = ctx.enter_context(tc.tile_pool(name="stores", bufs=8))
         psum_setup = ctx.enter_context(tc.psum_pool(name="psum_setup", bufs=1))
         psum_turn = ctx.enter_context(tc.psum_pool(name="psum_turn", bufs=2))
         psum_conv = ctx.enter_context(tc.psum_pool(name="psum_conv", bufs=3))
@@ -94,8 +99,8 @@ def tile_lablock_kernel(tc, x, w, conv_w, conv_b, out):
         for t in range(CB):
             nc.gpsimd.memset(x_cls[:, t].bitcast(I32), 0)
 
-        w_f32 = keep.tile([P, len(HORIZONTAL), CB, KT * KT], F32)
-        w_dup = keep.tile([P, len(VERTICAL), CB * KT * KT, B], BF16)
+        w_f32 = keep.tile([P, len(SHORT), CB, KT * KT], F32)
+        w_dup = keep.tile([P, CB * KT * KT, B], BF16)
 
         def weights_of(n):
             return w_bf[:, n, 0 : CB * KT * KT]
@@ -109,7 +114,8 @@ def tile_lablock_kernel(tc, x, w, conv_w, conv_b, out):
             ]
 
         def sort_rows(r, t):
-            copy = nc.scalar.copy if t in SCALAR_SORTS else nc.vector.tensor_copy
+            on_scalar = t in SCALAR_SORTS or (t == SCALAR_LATE and 1 < r < KT - 1)
+            copy = nc.scalar.copy if on_scalar else nc.vector.tensor_copy
             na = rows_of(r)
             full_q = W - (KCOLS - 1) * KT
             for b in range(B):
@@ -124,7 +130,7 @@ def tile_lablock_kernel(tc, x, w, conv_w, conv_b, out):
                 copy(out=dst[:, 0:full_q], in_=src[:, 0:full_q])
                 copy(out=dst[:, full_q:KT, :, 0 : KCOLS - 1], in_=src[:, full_q:KT, :, 0 : KCOLS - 1])
 
-        products = keep.tile([P, TAPS, CB, RING], F32)
+        products = keep.tile([P, len(SLOTS), CB, RING], F32)
         x1_codes = keep.tile([P, NPOS], U32, align_bytes=64)
         x1_scales = keep.tile([P, NPOS], U8, align_bytes=64)
 
@@ -141,6 +147,9 @@ def tile_lablock_kernel(tc, x, w, conv_w, conv_b, out):
             edge = (lo // RING + 1) * RING
             return [(lo, hi)] if hi <= edge else [(lo, edge), (edge, hi)]
 
+        def weight(n, t, r, q):
+            return w_f32[:, SHORT.index(n), t, r * KT + q : r * KT + q + 1]
+
         def multiply_on_scalar(r, q):
             sources = {
                 LEFT: class_start(r, (q - 1) % KT) + (q - 1) // KT,
@@ -149,64 +158,88 @@ def tile_lablock_kernel(tc, x, w, conv_w, conv_b, out):
             start = class_start(r, q)
             for lo, hi in ring_pieces(start, start + class_size(r)):
                 for t in range(CB):
-                    for slot, n in enumerate(HORIZONTAL):
+                    for n in (BASE, SIDE):
                         at = sources[n] + lo - start
                         nc.scalar.activation(
-                            out=products[:, SLOT[n], t, lo % RING : lo % RING + hi - lo],
+                            out=products[:, SLOTS[n], t, lo % RING : lo % RING + hi - lo],
                             in_=x_cls[:, t, at : at + hi - lo],
                             func=ACT.Copy,
-                            scale=w_f32[:, slot, t, r * KT + q : r * KT + q + 1],
+                            scale=weight(n, t, r, q),
                         )
 
         def unit(r):
             return rows_of(r) * KCOLS
 
-        def parts_of_group(r):
+        def parts(r, h_first, h_last):
             size = unit(r)
-            cut = RING - group_start(r) % RING
-            if cut >= KT * class_size(r):
-                return [(0, KT * B, 0, size)]
-            h, z = divmod(cut, size)
-            parts = [(0, h, 0, size), (h, 1, 0, z), (h, 1, z, size), (h + 1, KT * B - h - 1, 0, size)]
-            return [part for part in parts if part[1] > 0 and part[2] < part[3]]
+            h, z = divmod(RING - group_start(r) % RING, size)
+            if not h_first <= h < h_last:
+                return [(h_first, h_last - h_first, 0, size)]
+            runs = [(h_first, h - h_first, 0, size), (h, 1, 0, z), (h, 1, z, size), (h + 1, h_last - h - 1, 0, size)]
+            return [run for run in runs if run[1] > 0 and run[2] < run[3]]
+
+        def ring_start(r, h, z):
+            return (group_start(r) + h * unit(r) + z) % RING - z
 
         def columns(tile, ts, start, count, size, lo, hi):
             if count == 1:
                 return tile[:, ts, start + lo : start + hi]
             return tile[:, ts, start : start + count * size].rearrange("p t (h z) -> p t h z", z=size)[:, :, :, lo:hi]
 
+        def neighbour(r, step):
+            r2 = (r + step) % KT
+            moved = (r + step) // KT * KCOLS
+            return r2, moved, max(0, -moved), min(unit(r), unit(r2) - moved)
+
         def vector_products(r):
             size = unit(r)
             jobs = []
-            for n, step in ((UP, -1), (CENTRE, 0), (DOWN, 1)):
-                r2 = (r + step) % KT
-                moved = (r + step) // KT * KCOLS
-                product = products[:, SLOT[n]]
-                w_rows = w_dup[:, SLOT[n]].rearrange("p (t r q) b -> p t r (q b)", t=CB, r=KT)
-                inside_lo, inside_hi = max(0, -moved), min(size, unit(r2) - moved)
-                for h, count, z_lo, z_hi in parts_of_group(r):
-                    at = (group_start(r) + h * size + z_lo) % RING - z_lo
-                    at2 = group_start(r2) + h * unit(r2)
-                    lo, hi = max(z_lo, inside_lo), min(z_hi, inside_hi)
-                    for t in range(0, CB, 2):
-                        ts = slice(t, t + 2)
-                        weights = w_rows[:, ts, r, h : h + count]
-                        if count == 1:
-                            weights = weights.to_broadcast([P, 2, hi - lo])
-                        else:
-                            weights = weights.unsqueeze(3).to_broadcast([P, 2, count, hi - lo])
-                        for lo_out, hi_out in ((z_lo, min(z_hi, inside_lo)), (max(z_lo, inside_hi), z_hi)):
-                            if lo_out < hi_out:
-                                jobs.append((columns(product, ts, at, count, size, lo_out, hi_out), None, None))
-                        if lo < hi:
-                            jobs.append(
-                                (
-                                    columns(product, ts, at, count, size, lo, hi),
-                                    columns(x_cls, ts, at2, count, unit(r2), lo + moved, hi + moved),
-                                    weights,
-                                )
+            r2, moved, inside_lo, inside_hi = neighbour(r, 1)
+            product = products[:, SLOTS[WHOLE]]
+            w_rows = w_dup[:].rearrange("p (t r q) b -> p t r (q b)", t=CB, r=KT)
+            for h, count, z_lo, z_hi in parts(r, 0, KT * B):
+                at = ring_start(r, h, z_lo)
+                at2 = group_start(r2) + h * unit(r2)
+                lo, hi = max(z_lo, inside_lo), min(z_hi, inside_hi)
+                for t in range(0, CB, 2):
+                    ts = slice(t, t + 2)
+                    weights = w_rows[:, ts, r, h : h + count]
+                    if count == 1:
+                        weights = weights.to_broadcast([P, 2, hi - lo])
+                    else:
+                        weights = weights.unsqueeze(3).to_broadcast([P, 2, count, hi - lo])
+                    if inside_hi < z_hi:
+                        gap = max(z_lo, inside_hi)
+                        jobs.append((columns(product, ts, at, count, size, gap, z_hi), None, None))
+                    if lo < hi:
+                        jobs.append(
+                            (
+                                columns(product, ts, at, count, size, lo, hi),
+                                columns(x_cls, ts, at2, count, unit(r2), lo + moved, hi + moved),
+                                weights,
                             )
+                        )
             return jobs
+
+        def add_tap(n, r, q):
+            r2, moved, inside_lo, inside_hi = neighbour(r, {CENTRE: 0, UP: -1}[n])
+            for h, count, z_lo, z_hi in parts(r, q * B, (q + 1) * B):
+                at = ring_start(r, h, z_lo)
+                at2 = group_start(r2) + h * unit(r2)
+                lo, hi = max(z_lo, inside_lo), min(z_hi, inside_hi)
+                if lo >= hi:
+                    continue
+                for t in range(CB):
+                    ts = slice(t, t + 1)
+                    total = columns(products[:, SLOTS[BASE]], ts, at, count, unit(r), lo, hi)[:, 0]
+                    nc.vector.scalar_tensor_tensor(
+                        out=total,
+                        in0=columns(x_cls, ts, at2, count, unit(r2), lo + moved, hi + moved)[:, 0],
+                        scalar=weight(n, t, r, q),
+                        in1=total,
+                        op0=ALU.mult,
+                        op1=ALU.add,
+                    )
 
         def multiply_on_vector(job):
             product, x_moved, weights = job
@@ -219,10 +252,10 @@ def tile_lablock_kernel(tc, x, w, conv_w, conv_b, out):
             at = index * P % RING
             logits_t = psum_turn.tile([P, CB, P], F32, tag="logits_t")
             for t in range(CB):
-                for slot in range(TAPS):
+                for slot in range(len(SLOTS)):
                     nc.tensor.matmul(
                         out=logits_t[:, t, :], lhsT=products[:, slot, t, at : at + P], rhs=ident_f32[:],
-                        is_transpose=True, start=(slot == 0), stop=(slot == TAPS - 1),
+                        is_transpose=True, start=(slot == 0), stop=(slot == len(SLOTS) - 1),
                     )
             logits_t_of[index] = logits_t
 
@@ -258,7 +291,8 @@ def tile_lablock_kernel(tc, x, w, conv_w, conv_b, out):
 
         def make_gain(index):
             gain = gain_of[index]
-            nc.gpsimd.tensor_scalar(
+            engine = nc.gpsimd if index < NTILES - 2 else nc.vector
+            engine.tensor_scalar(
                 out=gain[:],
                 in0=gain[:],
                 scalar1=inv_total_of[index][:, 0:1],
@@ -277,9 +311,9 @@ def tile_lablock_kernel(tc, x, w, conv_w, conv_b, out):
             cols = slice(index * P, (index + 1) * P)
             x1_grouped = work.tile([P, P, CB], BF16, tag="x1_grouped", align_bytes=64)
             nc.vector.tensor_tensor(
-                out=x1_grouped[:],
-                in0=gain_c_of[index][:].rearrange("p t s -> p s t"),
-                in1=x_cls[:, :, cols].rearrange("p t s -> p s t"),
+                out=x1_grouped[:].rearrange("p (c s) t -> p c t s", s=NEAR),
+                in0=gain_c_of[index][:].rearrange("p t (c s) -> p c t s", s=NEAR),
+                in1=x_cls[:, :, cols].rearrange("p t (c s) -> p c t s", s=NEAR),
                 op=ALU.mult,
             )
             x1_of[index] = x1_grouped
@@ -314,28 +348,22 @@ def tile_lablock_kernel(tc, x, w, conv_w, conv_b, out):
             na = rows_of(r)
             inside = group_start(r) - window_start(r)
             by_class = conv_of[(r, ob)][:, inside : inside + KT * class_size(r)].rearrange(
-                "p (q b a k) -> p b a k q", q=KT, b=B, a=na
+                "p (q z k) -> p z k q", q=KT, k=KCOLS
             )
+            rows = stores.tile([P, B * rows_of(0), WPAD], F32, tag="rows")
+            in_order = rows[:, 0 : B * na, :].rearrange("p z (k q) -> p z k q", q=KT)
+            if on_vector:
+                nc.vector.tensor_scalar(
+                    out=in_order, in0=by_class, scalar1=bias[:, ob : ob + 1], scalar2=None, op0=ALU.add
+                )
+            else:
+                nc.scalar.activation(
+                    out=in_order, in_=by_class, func=ACT.Identity, bias=bias[:, ob : ob + 1], scale=1.0
+                )
             for b in range(B):
-                rows = stores.tile([P, rows_of(0), WPAD], F32, tag="rows")
-                in_order = rows[:, 0:na, :].rearrange("p a (k q) -> p a k q", q=KT)
-                if on_vector:
-                    nc.vector.tensor_scalar(
-                        out=in_order,
-                        in0=by_class[:, b],
-                        scalar1=bias[:, ob : ob + 1],
-                        scalar2=None,
-                        op0=ALU.add,
-                    )
-                else:
-                    nc.scalar.activation(
-                        out=in_order,
-                        in_=by_class[:, b],
-                        func=ACT.Identity,
-                        bias=bias[:, ob : ob + 1],
-                        scale=1.0,
-                    )
-                nc.sync.dma_start(out=out[b, ob * P : (ob + 1) * P, r:H:KT, :], in_=rows[:, 0:na, 0:W])
+                nc.sync.dma_start(
+                    out=out[b, ob * P : (ob + 1) * P, r:H:KT, :], in_=rows[:, b * na : (b + 1) * na, 0:W]
+                )
 
         cw_codes = keep.tile([P, O], U32, align_bytes=64)
         cw_scales = keep.tile([P, O], U8, align_bytes=64)
@@ -366,12 +394,11 @@ def tile_lablock_kernel(tc, x, w, conv_w, conv_b, out):
         def running(index):
             return 0 <= index < NTILES
 
-        for slot, n in enumerate(HORIZONTAL):
+        for slot, n in enumerate(SHORT):
             nc.scalar.copy(out=w_f32[:, slot].rearrange("p t z -> p (t z)"), in_=weights_of(n))
-        for slot, n in enumerate(VERTICAL):
-            nc.vector.tensor_copy(
-                out=w_dup[:, slot], in_=weights_of(n).unsqueeze(2).to_broadcast([P, CB * KT * KT, B])
-            )
+        nc.vector.tensor_copy(
+            out=w_dup[:], in_=weights_of(WHOLE).unsqueeze(2).to_broadcast([P, CB * KT * KT, B])
+        )
 
         sorts, products_at = {}, {}
         for r in range(KT):
@@ -412,13 +439,17 @@ def tile_lablock_kernel(tc, x, w, conv_w, conv_b, out):
                     store(r, ob, on_vector=False)
                 if step == OB + 1:
                     quantise_conv_w()
-                if running(step - 4):
-                    quantise(step - 4)
-                prepare(step)
-                multiply(step, 0)
                 if running(step - 3):
                     make_x1(step - 3)
+                prepare(step)
+                multiply(step, 0)
+                for r, q in classes_of(step + 1):
+                    add_tap(ADDED[0], r, q)
+                if running(step - 3):
+                    quantise(step - 3)
                 multiply(step, 1)
+                for r, q in classes_of(step + 1):
+                    add_tap(ADDED[1], r, q)
                 if running(step):
                     turn_logits(step)
                 if running(step - 2):
@@ -427,7 +458,7 @@ def tile_lablock_kernel(tc, x, w, conv_w, conv_b, out):
                     turn_conv_w(step - 1)
                 if step == OB + 1:
                     turn_bias()
-                while groups_seen < KT and window_start(groups_seen) + MX_N <= (step - 3) * P:
+                while groups_seen < KT and window_start(groups_seen) + MX_N <= (step - 2) * P:
                     waiting.extend((groups_seen, ob) for ob in range(OB))
                     groups_seen += 1
             for r, ob in waiting:

from contextlib import ExitStack

import concourse.mybir as mybir
from concourse.masks import make_identity

BF16 = mybir.dt.bfloat16
F32 = mybir.dt.float32
I32 = mybir.dt.int32
U32 = mybir.dt.uint32
U8 = mybir.dt.uint8
FP8X4 = mybir.dt.float8_e4m3fn_x4
ALU = mybir.AluOpType
ACT = mybir.ActivationFunctionType
AXIS = mybir.AxisListType

P = 128
B, C, O, H, W, KT = 2, 512, 512, 32, 40, 7
CB = C // P
OB = O // P
IMG = H * W
KCOLS = (W + KT - 1) // KT
WPAD = KCOLS * KT
MX_N = 512
ALIGN = 64

TAPS = 5
CENTRE, UP, DOWN, LEFT, RIGHT = range(TAPS)
BASE = LEFT
ADDED = (CENTRE, UP)
SIDE = RIGHT
WHOLE = DOWN
SHORT = (BASE, SIDE) + ADDED
SLOTS = {WHOLE: 0, BASE: 1, SIDE: 2}

FLOPS = 2 * B * IMG * C * O


def rows_of(r):
    return (H - r + KT - 1) // KT


def class_size(r):
    return B * rows_of(r) * KCOLS


def group_start(r):
    return sum(KT * class_size(rr) for rr in range(r))


def class_start(r, q):
    return group_start(r) + q * class_size(r)


NPOS = B * H * WPAD
NTILES = NPOS // P
LEAD = 2
CONV_PER_STEP = 2
W_ROOM = 208
RING = 10 * P
SCALAR_SORTS = (1, 3)
SCALAR_LATE = 2
NEAR = 4
XROOM = (H + KT - 1) * W


def tile_lablock_kernel(tc, x, w, conv_w, conv_b, out):
    nc = tc.nc
    with ExitStack() as ctx:
        keep = ctx.enter_context(tc.tile_pool(name="keep", bufs=1))
        work = ctx.enter_context(tc.tile_pool(name="work", bufs=4))
        small = ctx.enter_context(tc.tile_pool(name="small", bufs=4))
        stores = ctx.enter_context(tc.tile_pool(name="stores", bufs=8))
        psum_setup = ctx.enter_context(tc.psum_pool(name="psum_setup", bufs=1))
        psum_turn = ctx.enter_context(tc.psum_pool(name="psum_turn", bufs=2))
        psum_conv = ctx.enter_context(tc.psum_pool(name="psum_conv", bufs=3))

        x_img = keep.tile([P, CB, B, XROOM], BF16)
        for t in range(CB):
            nc.sync.dma_start(
                out=x_img[:, t, :, 0:IMG],
                in_=x.rearrange("b (p t) i j -> t p b (i j)", t=CB)[t],
            )
        w_bf = keep.tile([P, TAPS, W_ROOM], BF16)
        nc.scalar.dma_start(
            out=w_bf[:, :, 0 : CB * KT * KT], in_=w.rearrange("n (p t) r q -> p n (t r q)", p=P)
        )
        cw_rows = keep.tile([P, OB, C], BF16)
        nc.sync.dma_start(out=cw_rows[:], in_=conv_w.rearrange("(ob p) c -> p ob c", p=P))
        bias_rows = keep.tile([P, P], BF16)
        nc.vector.memset(bias_rows[:], 0.0)
        nc.sync.dma_start(out=bias_rows[0:OB, :], in_=conv_b.rearrange("(ob p) -> ob p", p=P))

        ident_f32 = keep.tile([P, P], F32)
        make_identity(nc, ident_f32[:])
        ident_bf = keep.tile([P, P], BF16)
        make_identity(nc, ident_bf[:])

        x_cls = keep.tile([P, CB, NPOS], BF16)
        for t in range(CB):
            nc.gpsimd.memset(x_cls[:, t].bitcast(I32), 0)

        w_f32 = keep.tile([P, len(SHORT), CB, KT * KT], F32)
        w_dup = keep.tile([P, CB * KT * KT, B], BF16)

        def weights_of(n):
            return w_bf[:, n, 0 : CB * KT * KT]

        def classes_of(index):
            return [
                (r, q)
                for r in range(KT)
                for q in range(KT)
                if index * P <= class_start(r, q) < (index + 1) * P
            ]

        def sort_rows(r, t):
            on_scalar = t in SCALAR_SORTS or (t == SCALAR_LATE and 1 < r < KT - 1)
            copy = nc.scalar.copy if on_scalar else nc.vector.tensor_copy
            na = rows_of(r)
            full_q = W - (KCOLS - 1) * KT
            for b in range(B):
                src = (
                    x_img[:, t, b, r * W : r * W + KT * W * na]
                    .rearrange("p (a z) -> p a z", z=KT * W)[:, :, 0:WPAD]
                    .rearrange("p a (k q) -> p q a k", q=KT)
                )
                dst = x_cls[:, t, group_start(r) : group_start(r + 1)].rearrange(
                    "p (q b a k) -> p q b a k", q=KT, b=B, a=na
                )[:, :, b]
                copy(out=dst[:, 0:full_q], in_=src[:, 0:full_q])
                copy(out=dst[:, full_q:KT, :, 0 : KCOLS - 1], in_=src[:, full_q:KT, :, 0 : KCOLS - 1])

        products = keep.tile([P, len(SLOTS), CB, RING], F32)
        x1_codes = keep.tile([P, NPOS], U32, align_bytes=64)
        x1_scales = keep.tile([P, NPOS], U8, align_bytes=64)

        logits_t_of = {}
        neg_max_of = {}
        gain_of = {}
        total_of = {}
        inv_total_of = {}
        gain_c_of = {}
        conv_of = {}
        x1_of = {}

        def ring_pieces(lo, hi):
            edge = (lo // RING + 1) * RING
            return [(lo, hi)] if hi <= edge else [(lo, edge), (edge, hi)]

        def weight(n, t, r, q):
            return w_f32[:, SHORT.index(n), t, r * KT + q : r * KT + q + 1]

        def multiply_on_scalar(r, q):
            sources = {
                LEFT: class_start(r, (q - 1) % KT) + (q - 1) // KT,
                RIGHT: class_start(r, (q + 1) % KT) + (q + 1) // KT,
            }
            start = class_start(r, q)
            for lo, hi in ring_pieces(start, start + class_size(r)):
                for t in range(CB):
                    for n in (BASE, SIDE):
                        at = sources[n] + lo - start
                        nc.scalar.activation(
                            out=products[:, SLOTS[n], t, lo % RING : lo % RING + hi - lo],
                            in_=x_cls[:, t, at : at + hi - lo],
                            func=ACT.Copy,
                            scale=weight(n, t, r, q),
                        )

        def unit(r):
            return rows_of(r) * KCOLS

        def parts(r, h_first, h_last):
            size = unit(r)
            h, z = divmod(RING - group_start(r) % RING, size)
            if not h_first <= h < h_last:
                return [(h_first, h_last - h_first, 0, size)]
            runs = [(h_first, h - h_first, 0, size), (h, 1, 0, z), (h, 1, z, size), (h + 1, h_last - h - 1, 0, size)]
            return [run for run in runs if run[1] > 0 and run[2] < run[3]]

        def ring_start(r, h, z):
            return (group_start(r) + h * unit(r) + z) % RING - z

        def columns(tile, ts, start, count, size, lo, hi):
            if count == 1:
                return tile[:, ts, start + lo : start + hi]
            return tile[:, ts, start : start + count * size].rearrange("p t (h z) -> p t h z", z=size)[:, :, :, lo:hi]

        def neighbour(r, step):
            r2 = (r + step) % KT
            moved = (r + step) // KT * KCOLS
            return r2, moved, max(0, -moved), min(unit(r), unit(r2) - moved)

        def vector_products(r):
            size = unit(r)
            jobs = []
            r2, moved, inside_lo, inside_hi = neighbour(r, 1)
            product = products[:, SLOTS[WHOLE]]
            w_rows = w_dup[:].rearrange("p (t r q) b -> p t r (q b)", t=CB, r=KT)
            for h, count, z_lo, z_hi in parts(r, 0, KT * B):
                at = ring_start(r, h, z_lo)
                at2 = group_start(r2) + h * unit(r2)
                lo, hi = max(z_lo, inside_lo), min(z_hi, inside_hi)
                for t in range(0, CB, 2):
                    ts = slice(t, t + 2)
                    weights = w_rows[:, ts, r, h : h + count]
                    if count == 1:
                        weights = weights.to_broadcast([P, 2, hi - lo])
                    else:
                        weights = weights.unsqueeze(3).to_broadcast([P, 2, count, hi - lo])
                    if inside_hi < z_hi:
                        gap = max(z_lo, inside_hi)
                        jobs.append((columns(product, ts, at, count, size, gap, z_hi), None, None))
                    if lo < hi:
                        jobs.append(
                            (
                                columns(product, ts, at, count, size, lo, hi),
                                columns(x_cls, ts, at2, count, unit(r2), lo + moved, hi + moved),
                                weights,
                            )
                        )
            return jobs

        def add_tap(n, r, q):
            r2, moved, inside_lo, inside_hi = neighbour(r, {CENTRE: 0, UP: -1}[n])
            for h, count, z_lo, z_hi in parts(r, q * B, (q + 1) * B):
                at = ring_start(r, h, z_lo)
                at2 = group_start(r2) + h * unit(r2)
                lo, hi = max(z_lo, inside_lo), min(z_hi, inside_hi)
                if lo >= hi:
                    continue
                for t in range(CB):
                    ts = slice(t, t + 1)
                    total = columns(products[:, SLOTS[BASE]], ts, at, count, unit(r), lo, hi)[:, 0]
                    nc.vector.scalar_tensor_tensor(
                        out=total,
                        in0=columns(x_cls, ts, at2, count, unit(r2), lo + moved, hi + moved)[:, 0],
                        scalar=weight(n, t, r, q),
                        in1=total,
                        op0=ALU.mult,
                        op1=ALU.add,
                    )

        def multiply_on_vector(job):
            product, x_moved, weights = job
            if weights is None:
                nc.vector.memset(product, 0.0)
            else:
                nc.vector.tensor_tensor(out=product, in0=x_moved, in1=weights, op=ALU.mult)

        def turn_logits(index):
            at = index * P % RING
            logits_t = psum_turn.tile([P, CB, P], F32, tag="logits_t")
            for t in range(CB):
                for slot in range(len(SLOTS)):
                    nc.tensor.matmul(
                        out=logits_t[:, t, :], lhsT=products[:, slot, t, at : at + P], rhs=ident_f32[:],
                        is_transpose=True, start=(slot == 0), stop=(slot == len(SLOTS) - 1),
                    )
            logits_t_of[index] = logits_t

        def find_max(index):
            neg_max = small.tile([P, 1], F32, tag="neg_max")
            nc.vector.tensor_reduce(
                out=neg_max[:],
                in_=logits_t_of[index][:].rearrange("p t c -> p (t c)"),
                axis=AXIS.X,
                op=ALU.max,
                negate=True,
            )
            neg_max_of[index] = neg_max

        def exponentials(index):
            gain = work.tile([P, C], F32, tag="gain")
            total = small.tile([P, 1], F32, tag="total")
            nc.scalar.activation(
                out=gain[:],
                in_=logits_t_of[index][:].rearrange("p t c -> p (t c)"),
                func=ACT.Exp,
                bias=neg_max_of[index][:, 0:1],
                scale=1.0,
                accum_out=total[:, 0:1],
            )
            gain_of[index] = gain
            total_of[index] = total

        def invert_total(index):
            inv_total = small.tile([P, 1], F32, tag="inv_total")
            nc.vector.reciprocal(inv_total[:], total_of[index][:])
            inv_total_of[index] = inv_total

        def make_gain(index):
            gain = gain_of[index]
            engine = nc.gpsimd if index < NTILES - 2 else nc.vector
            engine.tensor_scalar(
                out=gain[:],
                in0=gain[:],
                scalar1=inv_total_of[index][:, 0:1],
                scalar2=1.0,
                op0=ALU.mult,
                op1=ALU.add,
            )

        def turn_gain(index):
            gain_c = psum_turn.tile([P, CB, P], F32, tag="gain_c")
            for t in range(CB):
                nc.tensor.transpose(gain_c[:, t, :], gain_of[index][:, t * P : (t + 1) * P], ident_f32[:])
            gain_c_of[index] = gain_c

        def make_x1(index):
            cols = slice(index * P, (index + 1) * P)
            x1_grouped = work.tile([P, P, CB], BF16, tag="x1_grouped", align_bytes=64)
            nc.vector.tensor_tensor(
                out=x1_grouped[:].rearrange("p (c s) t -> p c t s", s=NEAR),
                in0=gain_c_of[index][:].rearrange("p t (c s) -> p c t s", s=NEAR),
                in1=x_cls[:, :, cols].rearrange("p t (c s) -> p c t s", s=NEAR),
                op=ALU.mult,
            )
            x1_of[index] = x1_grouped

        def quantise(index):
            cols = slice(index * P, (index + 1) * P)
            nc.vector.quantize_mx(
                out=x1_codes[:, cols].bitcast(FP8X4),
                scales=x1_scales[:, cols],
                in_=x1_of[index][:].rearrange("p s t -> p (s t)"),
            )

        def window_start(r):
            end = -(-group_start(r + 1) // ALIGN) * ALIGN
            return max(0, end - MX_N)

        def convolve(r, ob):
            first = window_start(r)
            conv = psum_conv.tile([P, MX_N], F32, tag="conv")
            nc.tensor.matmul_mx(
                out=conv[:],
                lhsT=cw_codes[:, ob * P : (ob + 1) * P].bitcast(FP8X4),
                lhsT_scale=cw_scales[:, ob * P : (ob + 1) * P],
                rhs=x1_codes[:, first : first + MX_N].bitcast(FP8X4),
                rhs_scale=x1_scales[:, first : first + MX_N],
                start=True,
                stop=True,
            )
            conv_of[(r, ob)] = conv

        def store(r, ob, on_vector):
            na = rows_of(r)
            inside = group_start(r) - window_start(r)
            by_class = conv_of[(r, ob)][:, inside : inside + KT * class_size(r)].rearrange(
                "p (q z k) -> p z k q", q=KT, k=KCOLS
            )
            rows = stores.tile([P, B * rows_of(0), WPAD], F32, tag="rows")
            in_order = rows[:, 0 : B * na, :].rearrange("p z (k q) -> p z k q", q=KT)
            if on_vector:
                nc.vector.tensor_scalar(
                    out=in_order, in0=by_class, scalar1=bias[:, ob : ob + 1], scalar2=None, op0=ALU.add
                )
            else:
                nc.scalar.activation(
                    out=in_order, in_=by_class, func=ACT.Identity, bias=bias[:, ob : ob + 1], scale=1.0
                )
            for b in range(B):
                nc.sync.dma_start(
                    out=out[b, ob * P : (ob + 1) * P, r:H:KT, :], in_=rows[:, b * na : (b + 1) * na, 0:W]
                )

        cw_codes = keep.tile([P, O], U32, align_bytes=64)
        cw_scales = keep.tile([P, O], U8, align_bytes=64)
        bias = keep.tile([P, OB], F32)

        cw_grouped = keep.tile([P, O, CB], BF16, align_bytes=64)

        def turn_conv_w(ob):
            cw_turned = psum_setup.tile([P, CB, P], BF16, tag="setup", name="cw_turned")
            for t in range(CB):
                nc.tensor.transpose(cw_turned[:, t, :], cw_rows[:, ob, t:C:CB], ident_bf[:])
            nc.scalar.copy(
                out=cw_grouped[:, ob * P : (ob + 1) * P, :], in_=cw_turned[:].rearrange("p t o -> p o t")
            )

        def quantise_conv_w():
            nc.vector.quantize_mx(
                out=cw_codes[:].bitcast(FP8X4),
                scales=cw_scales[:],
                in_=cw_grouped[:].rearrange("p o t -> p (o t)"),
            )

        def turn_bias():
            bias_turned = psum_setup.tile([P, CB, P], BF16, tag="setup", name="bias_turned")
            nc.tensor.transpose(bias_turned[:, 0, :], bias_rows[:], ident_bf[:])
            nc.scalar.copy(out=bias[:], in_=bias_turned[:, 0, 0:OB])

        def running(index):
            return 0 <= index < NTILES

        for slot, n in enumerate(SHORT):
            nc.scalar.copy(out=w_f32[:, slot].rearrange("p t z -> p (t z)"), in_=weights_of(n))
        nc.vector.tensor_copy(
            out=w_dup[:], in_=weights_of(WHOLE).unsqueeze(2).to_broadcast([P, CB * KT * KT, B])
        )

        sorts, products_at = {}, {}
        for r in range(KT):
            first = group_start(r) // P
            jobs = vector_products(r)
            for k, job in enumerate(jobs):
                products_at.setdefault(first - 3 + 3 * k // len(jobs), []).append(job)
            for r_new in (KT - 1, 0, 1) if r == 0 else (r + 1,) if r + 1 < KT - 1 else ():
                for t in range(CB):
                    sorts.setdefault(first - 6 + min(t, 2), []).append((r_new, t))

        def prepare(step):
            for r, t in sorts.get(step, []):
                sort_rows(r, t)
            for r, q in classes_of(step + LEAD):
                multiply_on_scalar(r, q)

        def multiply(step, half):
            jobs = products_at.get(step, [])
            middle = (len(jobs) + 1) // 2
            for job in jobs[:middle] if half == 0 else jobs[middle:]:
                multiply_on_vector(job)

        with tc.manual_schedule():
            groups_seen = 0
            waiting = []
            for step in range(-6, NTILES + 5):
                blocks = waiting[0:CONV_PER_STEP]
                waiting = waiting[CONV_PER_STEP:]
                if running(step - 2):
                    invert_total(step - 2)
                    make_gain(step - 2)
                if running(step - 1):
                    find_max(step - 1)
                    exponentials(step - 1)
                for r, ob in blocks:
                    convolve(r, ob)
                    store(r, ob, on_vector=False)
                if step == OB + 1:
                    quantise_conv_w()
                if running(step - 3):
                    make_x1(step - 3)
                prepare(step)
                multiply(step, 0)
                for r, q in classes_of(step + 1):
                    add_tap(ADDED[0], r, q)
                if running(step - 3):
                    quantise(step - 3)
                multiply(step, 1)
                for r, q in classes_of(step + 1):
                    add_tap(ADDED[1], r, q)
                if running(step):
                    turn_logits(step)
                if running(step - 2):
                    turn_gain(step - 2)
                if 0 <= step - 1 < OB:
                    turn_conv_w(step - 1)
                if step == OB + 1:
                    turn_bias()
                while groups_seen < KT and window_start(groups_seen) + MX_N <= (step - 2) * P:
                    waiting.extend((groups_seen, ob) for ob in range(OB))
                    groups_seen += 1
            for r, ob in waiting:
                convolve(r, ob)
                store(r, ob, on_vector=(ob % 2 == 1))
